import numpy as np
import ml_dtypes


def mxq(x, axis, fmt="e4m3"):
    dtype, down = {"e4m3": (ml_dtypes.float8_e4m3fn, 7), "e5m2": (ml_dtypes.float8_e5m2, 14)}[fmt]
    v = np.moveaxis(np.asarray(x, np.float32).astype(ml_dtypes.bfloat16).astype(np.float64), axis, -1)
    blocks = v.reshape(v.shape[:-1] + (-1, 32))
    amax = np.abs(blocks).max(-1, keepdims=True)
    byte = np.maximum(np.where(amax > 0, np.frexp(amax)[1] - 1 + 127, 0) - down, 1)
    scale = np.exp2(byte - 127.0)
    codes = (blocks / scale).astype(np.float32).astype(dtype).astype(np.float64)
    return np.moveaxis((codes * scale).reshape(v.shape), -1, axis)


WIDE = False


def mx_kscale(k):
    if not WIDE:
        return np.ones(k)
    levels = np.array([10, -10, 5, -5, 0])
    a = np.random.permutation(np.resize(levels, k // 512 * 4)).reshape(k // 512, 4)
    idx = np.arange(k)
    return np.exp2(a[idx // 512, idx % 128 // 32])


BF16 = ml_dtypes.bfloat16


def bf(x):
    return np.asarray(x, np.float32).astype(BF16)


def f64(x):
    return np.asarray(x).astype(np.float64)


B, D, S, A, H, G = 4096, 512, 1024, 128, 512, 1
DG = D // G


def silu(v):
    return v / (1.0 + np.exp(-v))


def sigmoid(v):
    return 1.0 / (1.0 + np.exp(-v))


def setup_inputs():
    n = np.random.standard_normal
    t = mx_kscale(D)
    return {"y_dyn": bf(silu(n((B, D))) * t), "deter": bf(n((B, D))),
            "gru_W": bf(n((G, DG, 3 * DG)) * 2.0 / np.sqrt(DG) / t.reshape(G, DG)[:, :, None]), "gru_b": bf(n(3 * D) * 0.2)}


def reference(y_dyn, deter, gru_W, gru_b):
    yg = f64(y_dyn).reshape(B, G, DG).transpose(1, 0, 2)
    z = mxq(yg, 2, "e4m3") @ mxq(f64(gru_W), 1, "e4m3")
    z = z.transpose(1, 0, 2).reshape(B, 3 * D) + f64(gru_b)
    reset, cand, update = z[:, :D], z[:, D:2 * D], z[:, 2 * D:]
    reset = sigmoid(reset)
    cand = np.tanh(reset * cand)
    update = sigmoid(update - 1.0)
    return update * cand + (1.0 - update) * f64(deter)

@@ -1,0 +1,246 @@
+from contextlib import ExitStack
+
+import concourse.mybir as mybir
+from concourse.masks import make_identity
+
+FLOPS = 2 * 4096 * 512 * 1536
+
+F32 = mybir.dt.float32
+BF16 = mybir.dt.bfloat16
+U32 = mybir.dt.uint32
+U8 = mybir.dt.uint8
+FP8X4 = mybir.dt.float8_e4m3fn_x4
+ACT = mybir.ActivationFunctionType
+ALU = mybir.AluOpType
+
+P = 128
+N = 512
+ROUNDS = 8
+STRIPS = 4 * ROUNDS
+GATE_R, GATE_C, GATE_U = 0, 1, 2
+
+
+def tile_blockgrucell_pb_t_kernel(tc, y_dyn, deter, gru_W, gru_b, out):
+    nc = tc.nc
+    y_rows = y_dyn.rearrange("(g p i) k -> g p (i k)", p=P, i=4)
+    d_rows = deter.rearrange("(g p i) c -> g p (i c)", p=P, i=4)
+    o_rows = out.rearrange("(g p i) c -> g p i c", p=P, i=4)
+
+    with ExitStack() as ctx:
+        keep = ctx.enter_context(tc.tile_pool(name="keep", bufs=1))
+        work = ctx.enter_context(tc.tile_pool(name="work", bufs=3))
+        psum = ctx.enter_context(tc.psum_pool(name="psum", bufs=1))
+        ctx.enter_context(tc.manual_schedule())
+
+        def bank(tag, bufs):
+            return psum.tile([P, N], F32, name=tag, tag=tag, bufs=bufs)
+
+        def strip_tile(tag, bufs):
+            return work.tile([P, N], F32, name=tag, tag=tag, bufs=bufs)
+
+        ident = keep.tile([P, P], F32, name="ident")
+        make_identity(nc, ident[:])
+        b_rows = keep.tile([P, 256], BF16, name="b_rows")
+        nc.vector.memset(b_rows[:], 0.0)
+        nc.scalar.dma_start(out=b_rows[0:6, :], in_=gru_b.rearrange("(m c) -> m c", c=256))
+        warm = keep.tile([P, 2], F32, name="warm")
+        nc.vector.memset(warm[:], 0.0)
+        nc.scalar.activation(out=warm[:, 1:2], in_=warm[:, 0:1], func=ACT.Sigmoid)
+
+        y_sb = [keep.tile([P, 4 * 512], BF16, name="y%d" % g) for g in range(ROUNDS)]
+        d_sb = [keep.tile([P, 4 * 512], BF16, name="d%d" % g) for g in range(ROUNDS)]
+        w_raw = keep.tile([P, 4, 1536], BF16, name="w_raw")
+        for half in range(2):
+            cols = slice(1024 * half, 1024 * half + 1024)
+            nc.sync.dma_start(out=y_sb[0][:, cols], in_=y_rows[0][:, cols])
+        for h in range(2):
+            for gate in (GATE_R, GATE_U, GATE_C):
+                cols = slice(512 * gate + 256 * h, 512 * gate + 256 * h + 256)
+                for u in range(2):
+                    nc.sync.dma_start(
+                        out=w_raw[:, 2 * u : 2 * u + 2, cols],
+                        in_=gru_W[0, 256 * u : 256 * u + 256, cols].rearrange("(q j) c -> q j c", j=2),
+                    )
+        for g in range(ROUNDS):
+            if g + 1 < ROUNDS:
+                nc.sync.dma_start(out=y_sb[g + 1][:], in_=y_rows[g + 1])
+            nc.sync.dma_start(out=d_sb[g][:], in_=d_rows[g])
+
+        b_bank = bank("yT", 1)
+        nc.tensor.transpose(b_bank[:, 0:P], b_rows[:].bitcast(F32), ident[:])
+        bias = keep.tile([P, 12], F32, name="bias")
+        nc.vector.tensor_copy(out=bias[:], in_=b_bank[:].bitcast(BF16)[:, 0:12])
+        nc.vector.tensor_scalar_add(
+            out=bias[:, 4 * GATE_U : 4 * GATE_U + 4], in0=bias[:, 4 * GATE_U : 4 * GATE_U + 4], scalar1=-1.0
+        )
+
+        def bias_of(gate, x):
+            column = 4 * gate + x % 4
+            return bias[:, column : column + 1]
+
+        w_grouped = keep.tile([P, 6 * 1024], BF16, name="w_grouped", align_bytes=64)
+        w_codes = keep.tile([P, 6 * 256], U32, name="w_codes", align_bytes=64)
+        w_scales = keep.tile([P, 6 * 256], U8, name="w_scales", align_bytes=64)
+
+        def regroup_weights(copy, h, gate):
+            slot = 3 * h + gate
+            first = 512 * gate + 256 * h
+            copy(
+                out=w_grouped[:, 1024 * slot : 1024 * slot + 1024].rearrange("p (e q t) -> p e q t", e=2, t=4),
+                in_=w_raw[:, :, first : first + 256].rearrange("p t (q e) -> p e q t", e=2),
+            )
+
+        def quantise_weights(h, gate):
+            slot = 3 * h + gate
+            nc.vector.quantize_mx(
+                out=w_codes[:, 256 * slot : 256 * slot + 256].bitcast(FP8X4),
+                scales=w_scales[:, 256 * slot : 256 * slot + 256],
+                in_=w_grouped[:, 1024 * slot : 1024 * slot + 1024],
+            )
+
+        live = {}
+
+        def transpose_y(g, half):
+            live["yT", g, half] = bank("yT", 1)
+            words = y_sb[g][:].bitcast(F32)
+            for i in range(2):
+                for u in range(2):
+                    src = 256 * (2 * half + i) + 128 * u
+                    dst = 128 * (2 * i + u)
+                    nc.tensor.transpose(live["yT", g, half][:, dst : dst + P], words[:, src : src + P], ident[:])
+
+        def regroup_y(copy, g, half):
+            if half == 0:
+                live["y_grouped", g] = work.tile([P, 4 * N], BF16, name="y_grouped", tag="y_grouped", bufs=2, align_bytes=64)
+            words = live["y_grouped", g][:].bitcast(F32).rearrange("p (n u) -> p n u", u=2)
+            copy(
+                out=words[:, 256 * half : 256 * half + 256, :].rearrange("p (i r) u -> p i r u", i=2),
+                in_=live["yT", g, half][:].rearrange("p (i u r) -> p i r u", i=2, u=2),
+            )
+
+        def quantise_y(g):
+            live["y_codes", g] = work.tile([P, N], U32, name="y_codes", tag="y_codes", bufs=2, align_bytes=64)
+            live["y_scales", g] = work.tile([P, N], U8, name="y_scales", tag="y_scales", bufs=2, align_bytes=64)
+            nc.vector.quantize_mx(
+                out=live["y_codes", g][:].bitcast(FP8X4), scales=live["y_scales", g][:], in_=live["y_grouped", g][:]
+            )
+
+        def project(x):
+            g, h, e = x // 4, x // 2 % 2, x % 2
+            for gate in (GATE_R, GATE_U, GATE_C):
+                first = 256 * (3 * h + gate) + P * e
+                live["z", gate, x] = bank("z", 4)
+                nc.tensor.matmul_mx(
+                    out=live["z", gate, x][:],
+                    lhsT=w_codes[:, first : first + P].bitcast(FP8X4),
+                    lhsT_scale=w_scales[:, first : first + P],
+                    rhs=live["y_codes", g][:].bitcast(FP8X4),
+                    rhs_scale=live["y_scales", g][:],
+                    start=True,
+                    stop=True,
+                )
+
+        def gates(x):
+            live["reset", x] = strip_tile("reset", 3)
+            live["update", x] = strip_tile("update", 5)
+            live["product", x] = strip_tile("product", 3)
+            nc.scalar.activation(
+                out=live["reset", x][:], in_=live["z", GATE_R, x][:], func=ACT.Sigmoid, bias=bias_of(GATE_R, x)
+            )
+            nc.scalar.activation(
+                out=live["update", x][:], in_=live["z", GATE_U, x][:], func=ACT.Sigmoid, bias=bias_of(GATE_U, x)
+            )
+            nc.vector.scalar_tensor_tensor(
+                out=live["product", x][:],
+                in0=live["z", GATE_C, x][:],
+                scalar=bias_of(GATE_C, x),
+                in1=live["reset", x][:],
+                op0=ALU.add,
+                op1=ALU.mult,
+            )
+
+        def candidate(x):
+            live["cand", x] = strip_tile("cand", 3)
+            nc.scalar.activation(out=live["cand", x][:], in_=live["product", x][:], func=ACT.Tanh)
+
+        def transpose_deter(pair):
+            g, h = pair // 2, pair % 2
+            live["deterT", pair] = bank("deterT", 1)
+            words = d_sb[g][:].bitcast(F32)
+            for i in range(4):
+                src = 256 * i + P * h
+                nc.tensor.transpose(live["deterT", pair][:, P * i : P * i + P], words[:, src : src + P], ident[:])
+
+        def blend(x):
+            live["diff", x] = strip_tile("diff", 3)
+            live["step", x] = strip_tile("step", 5)
+            nc.vector.tensor_tensor(
+                out=live["diff", x][:],
+                in0=live["cand", x][:],
+                in1=live["deterT", x // 2][:].bitcast(BF16).rearrange("p (n e) -> p e n", e=2)[:, x % 2, :],
+                op=ALU.subtract,
+            )
+            engine = nc.vector if x == STRIPS - 1 else nc.gpsimd
+            engine.tensor_tensor(out=live["step", x][:], in0=live["update", x][:], in1=live["diff", x][:], op=ALU.mult)
+
+        def transpose_back(x):
+            even = x - x % 2
+            live["back", x] = bank("back", 2)
+            for i in range(2):
+                for e in range(2):
+                    src = P * (2 * (x % 2) + i)
+                    dst = P * (2 * i + e)
+                    nc.tensor.transpose(live["back", x][:, dst : dst + P], live["step", even + e][:, src : src + P], ident[:])
+
+        def finish(x):
+            g, h, slots = x // 4, x // 2 % 2, slice(2 * (x % 2), 2 * (x % 2) + 2)
+            cols = slice(256 * h, 256 * h + 256)
+            result = strip_tile("result", 4)
+            nc.vector.tensor_tensor(
+                out=result[:].rearrange("p (i q e) -> p i q e", i=2, e=2),
+                in0=live["back", x][:].rearrange("p (i e q) -> p i q e", i=2, e=2),
+                in1=d_sb[g][:].rearrange("p (i c) -> p i c", i=4)[:, slots, cols].rearrange("p i (q e) -> p i q e", e=2),
+                op=ALU.add,
+            )
+            nc.sync.dma_start(out=o_rows[g][:, slots, cols], in_=result[:].rearrange("p (i c) -> p i c", i=2))
+
+        transpose_y(0, 0)
+        regroup_y(nc.scalar.copy, 0, 0)
+        transpose_y(0, 1)
+        regroup_weights(nc.vector.tensor_copy, 0, GATE_R)
+        quantise_weights(0, GATE_R)
+        regroup_y(nc.scalar.copy, 0, 1)
+        quantise_y(0)
+        regroup_weights(nc.scalar.copy, 0, GATE_U)
+        regroup_weights(nc.vector.tensor_copy, 0, GATE_C)
+        quantise_weights(0, GATE_U)
+        quantise_weights(0, GATE_C)
+        for gate in (GATE_R, GATE_U, GATE_C):
+            regroup_weights(nc.vector.tensor_copy, 1, gate)
+            quantise_weights(1, gate)
+
+        def in_range(x):
+            return 0 <= x < STRIPS
+
+        for s in range(-2, STRIPS + 4):
+            if in_range(s - 1):
+                blend(s - 1)
+            if in_range(s - 4):
+                finish(s - 4)
+            if in_range(s + 1):
+                gates(s + 1)
+            if in_range(s):
+                candidate(s)
+            if in_range(s + 5) and s + 5 >= 4 and (s + 5) % 4 < 2:
+                half = (s + 5) % 4
+                regroup_y(nc.scalar.copy if half == 0 else nc.vector.tensor_copy, (s + 5) // 4, half)
+            if in_range(s + 4) and s + 4 >= 4 and (s + 4) % 4 == 0:
+                quantise_y((s + 4) // 4)
+            if in_range(s + 2):
+                project(s + 2)
+            if in_range(s) and s % 2 == 0:
+                transpose_deter(s // 2)
+            if in_range(s - 3):
+                transpose_back(s - 3)
+            if in_range(s + 6) and s + 6 >= 4 and (s + 6) % 4 < 2:
+                transpose_y((s + 6) // 4, (s + 6) % 4)

@@ -101,7 +101,7 @@ def tile_blockgrucell_pb_t_kernel(tc, y_dyn, deter, gru_W, gru_b, out):
         live = {}
 
         def transpose_y(g, half):
-            live["yT", g, half] = bank("yT", 1)
+            live["yT", g, half] = bank("back", 2) if g == 0 else bank("yT", 1)
             words = y_sb[g][:].bitcast(F32)
             for i in range(2):
                 for u in range(2):
@@ -109,11 +109,11 @@ def tile_blockgrucell_pb_t_kernel(tc, y_dyn, deter, gru_W, gru_b, out):
                     dst = 128 * (2 * i + u)
                     nc.tensor.transpose(live["yT", g, half][:, dst : dst + P], words[:, src : src + P], ident[:])
 
-        def regroup_y(copy, g, half):
+        def regroup_y(g, half):
             if half == 0:
                 live["y_grouped", g] = work.tile([P, 4 * N], BF16, name="y_grouped", tag="y_grouped", bufs=2, align_bytes=64)
             words = live["y_grouped", g][:].bitcast(F32).rearrange("p (n u) -> p n u", u=2)
-            copy(
+            nc.scalar.copy(
                 out=words[:, 256 * half : 256 * half + 256, :].rearrange("p (i r) u -> p i r u", i=2),
                 in_=live["yT", g, half][:].rearrange("p (i u r) -> p i r u", i=2, u=2),
             )
@@ -205,11 +205,11 @@ def tile_blockgrucell_pb_t_kernel(tc, y_dyn, deter, gru_W, gru_b, out):
             nc.sync.dma_start(out=o_rows[g][:, slots, cols], in_=result[:].rearrange("p (i c) -> p i c", i=2))
 
         transpose_y(0, 0)
-        regroup_y(nc.scalar.copy, 0, 0)
         transpose_y(0, 1)
+        regroup_y(0, 0)
+        regroup_y(0, 1)
         regroup_weights(nc.vector.tensor_copy, 0, GATE_R)
         quantise_weights(0, GATE_R)
-        regroup_y(nc.scalar.copy, 0, 1)
         quantise_y(0)
         regroup_weights(nc.scalar.copy, 0, GATE_U)
         regroup_weights(nc.vector.tensor_copy, 0, GATE_C)
@@ -225,22 +225,21 @@ def tile_blockgrucell_pb_t_kernel(tc, y_dyn, deter, gru_W, gru_b, out):
         for s in range(-2, STRIPS + 4):
             if in_range(s - 1):
                 blend(s - 1)
-            if in_range(s - 4):
-                finish(s - 4)
+            if 4 <= s + 3 < STRIPS and (s + 3) % 4 == 0:
+                quantise_y((s + 3) // 4)
             if in_range(s + 1):
                 gates(s + 1)
+            if 4 <= s + 5 < STRIPS and (s + 5) % 4 < 2:
+                regroup_y((s + 5) // 4, (s + 5) % 4)
+            if in_range(s - 4):
+                finish(s - 4)
             if in_range(s):
                 candidate(s)
-            if in_range(s + 5) and s + 5 >= 4 and (s + 5) % 4 < 2:
-                half = (s + 5) % 4
-                regroup_y(nc.scalar.copy if half == 0 else nc.vector.tensor_copy, (s + 5) // 4, half)
-            if in_range(s + 4) and s + 4 >= 4 and (s + 4) % 4 == 0:
-                quantise_y((s + 4) // 4)
             if in_range(s + 2):
                 project(s + 2)
+            if 4 <= s + 6 < STRIPS and (s + 6) % 4 < 2:
+                transpose_y((s + 6) // 4, (s + 6) % 4)
             if in_range(s) and s % 2 == 0:
                 transpose_deter(s // 2)
             if in_range(s - 3):
                 transpose_back(s - 3)
-            if in_range(s + 6) and s + 6 >= 4 and (s + 6) % 4 < 2:
-                transpose_y((s + 6) // 4, (s + 6) % 4)

@@ -30,7 +30,6 @@ def tile_blockgrucell_pb_t_kernel(tc, y_dyn, deter, gru_W, gru_b, out):
         keep = ctx.enter_context(tc.tile_pool(name="keep", bufs=1))
         work = ctx.enter_context(tc.tile_pool(name="work", bufs=3))
         psum = ctx.enter_context(tc.psum_pool(name="psum", bufs=1))
-        ctx.enter_context(tc.manual_schedule())
 
         def bank(tag, bufs):
             return psum.tile([P, N], F32, name=tag, tag=tag, bufs=bufs)

@@ -30,6 +30,7 @@ def tile_blockgrucell_pb_t_kernel(tc, y_dyn, deter, gru_W, gru_b, out):
         keep = ctx.enter_context(tc.tile_pool(name="keep", bufs=1))
         work = ctx.enter_context(tc.tile_pool(name="work", bufs=3))
         psum = ctx.enter_context(tc.psum_pool(name="psum", bufs=1))
+        ctx.enter_context(tc.manual_schedule())
 
         def bank(tag, bufs):
             return psum.tile([P, N], F32, name=tag, tag=tag, bufs=bufs)
@@ -108,11 +109,11 @@ def tile_blockgrucell_pb_t_kernel(tc, y_dyn, deter, gru_W, gru_b, out):
                     dst = 128 * (2 * i + u)
                     nc.tensor.transpose(live["yT", g, half][:, dst : dst + P], words[:, src : src + P], ident[:])
 
-        def regroup_y(g, half):
+        def regroup_y(copy, g, half):
             if half == 0:
                 live["y_grouped", g] = work.tile([P, 4 * N], BF16, name="y_grouped", tag="y_grouped", bufs=2, align_bytes=64)
             words = live["y_grouped", g][:].bitcast(F32).rearrange("p (n u) -> p n u", u=2)
-            nc.scalar.copy(
+            copy(
                 out=words[:, 256 * half : 256 * half + 256, :].rearrange("p (i r) u -> p i r u", i=2),
                 in_=live["yT", g, half][:].rearrange("p (i u r) -> p i r u", i=2, u=2),
             )
@@ -205,8 +206,8 @@ def tile_blockgrucell_pb_t_kernel(tc, y_dyn, deter, gru_W, gru_b, out):
 
         transpose_y(0, 0)
         transpose_y(0, 1)
-        regroup_y(0, 0)
-        regroup_y(0, 1)
+        regroup_y(nc.scalar.copy, 0, 0)
+        regroup_y(nc.scalar.copy, 0, 1)
         regroup_weights(nc.vector.tensor_copy, 0, GATE_R)
         quantise_weights(0, GATE_R)
         quantise_y(0)
@@ -222,16 +223,20 @@ def tile_blockgrucell_pb_t_kernel(tc, y_dyn, deter, gru_W, gru_b, out):
             return 0 <= x < STRIPS
 
         for s in range(-2, STRIPS + 4):
-            if in_range(s - 1):
-                blend(s - 1)
+            next_round, j = divmod(s + 5, 4)
+            copy_y = 1 <= next_round < ROUNDS and j < 2
             if 4 <= s + 3 < STRIPS and (s + 3) % 4 == 0:
                 quantise_y((s + 3) // 4)
+            if in_range(s - 1):
+                blend(s - 1)
+            if copy_y and j == 1:
+                regroup_y(nc.vector.tensor_copy, next_round, 1)
             if in_range(s + 1):
                 gates(s + 1)
-            if 4 <= s + 5 < STRIPS and (s + 5) % 4 < 2:
-                regroup_y((s + 5) // 4, (s + 5) % 4)
             if in_range(s - 4):
                 finish(s - 4)
+            if copy_y and j == 0:
+                regroup_y(nc.scalar.copy, next_round, 0)
             if in_range(s):
                 candidate(s)
             if in_range(s + 2):

@@ -225,10 +225,10 @@ def tile_blockgrucell_pb_t_kernel(tc, y_dyn, deter, gru_W, gru_b, out):
         for s in range(-2, STRIPS + 4):
             next_round, j = divmod(s + 5, 4)
             copy_y = 1 <= next_round < ROUNDS and j < 2
-            if 4 <= s + 3 < STRIPS and (s + 3) % 4 == 0:
-                quantise_y((s + 3) // 4)
             if in_range(s - 1):
                 blend(s - 1)
+            if 4 <= s + 3 < STRIPS and (s + 3) % 4 == 0:
+                quantise_y((s + 3) // 4)
             if copy_y and j == 1:
                 regroup_y(nc.vector.tensor_copy, next_round, 1)
             if in_range(s + 1):

@@ -109,11 +109,11 @@ def tile_blockgrucell_pb_t_kernel(tc, y_dyn, deter, gru_W, gru_b, out):
                     dst = 128 * (2 * i + u)
                     nc.tensor.transpose(live["yT", g, half][:, dst : dst + P], words[:, src : src + P], ident[:])
 
-        def regroup_y(copy, g, half):
+        def regroup_y(g, half):
             if half == 0:
                 live["y_grouped", g] = work.tile([P, 4 * N], BF16, name="y_grouped", tag="y_grouped", bufs=2, align_bytes=64)
             words = live["y_grouped", g][:].bitcast(F32).rearrange("p (n u) -> p n u", u=2)
-            copy(
+            nc.scalar.copy(
                 out=words[:, 256 * half : 256 * half + 256, :].rearrange("p (i r) u -> p i r u", i=2),
                 in_=live["yT", g, half][:].rearrange("p (i u r) -> p i r u", i=2, u=2),
             )
@@ -180,7 +180,7 @@ def tile_blockgrucell_pb_t_kernel(tc, y_dyn, deter, gru_W, gru_b, out):
                 in1=live["deterT", x // 2][:].bitcast(BF16).rearrange("p (n e) -> p e n", e=2)[:, x % 2, :],
                 op=ALU.subtract,
             )
-            engine = nc.vector if x == STRIPS - 1 else nc.gpsimd
+            engine = nc.vector if x % 4 == 3 else nc.gpsimd
             engine.tensor_tensor(out=live["step", x][:], in0=live["update", x][:], in1=live["diff", x][:], op=ALU.mult)
 
         def transpose_back(x):
@@ -206,8 +206,8 @@ def tile_blockgrucell_pb_t_kernel(tc, y_dyn, deter, gru_W, gru_b, out):
 
         transpose_y(0, 0)
         transpose_y(0, 1)
-        regroup_y(nc.scalar.copy, 0, 0)
-        regroup_y(nc.scalar.copy, 0, 1)
+        regroup_y(0, 0)
+        regroup_y(0, 1)
         regroup_weights(nc.vector.tensor_copy, 0, GATE_R)
         quantise_weights(0, GATE_R)
         quantise_y(0)
@@ -223,20 +223,16 @@ def tile_blockgrucell_pb_t_kernel(tc, y_dyn, deter, gru_W, gru_b, out):
             return 0 <= x < STRIPS
 
         for s in range(-2, STRIPS + 4):
-            next_round, j = divmod(s + 5, 4)
-            copy_y = 1 <= next_round < ROUNDS and j < 2
             if in_range(s - 1):
                 blend(s - 1)
             if 4 <= s + 3 < STRIPS and (s + 3) % 4 == 0:
                 quantise_y((s + 3) // 4)
-            if copy_y and j == 1:
-                regroup_y(nc.vector.tensor_copy, next_round, 1)
             if in_range(s + 1):
                 gates(s + 1)
+            if 4 <= s + 5 < STRIPS and (s + 5) % 4 < 2:
+                regroup_y((s + 5) // 4, (s + 5) % 4)
             if in_range(s - 4):
                 finish(s - 4)
-            if copy_y and j == 0:
-                regroup_y(nc.scalar.copy, next_round, 0)
             if in_range(s):
                 candidate(s)
             if in_range(s + 2):

@@ -118,11 +118,15 @@ def tile_blockgrucell_pb_t_kernel(tc, y_dyn, deter, gru_W, gru_b, out):
                 in_=live["yT", g, half][:].rearrange("p (i u r) -> p i r u", i=2, u=2),
             )
 
-        def quantise_y(g):
-            live["y_codes", g] = work.tile([P, N], U32, name="y_codes", tag="y_codes", bufs=2, align_bytes=64)
-            live["y_scales", g] = work.tile([P, N], U8, name="y_scales", tag="y_scales", bufs=2, align_bytes=64)
+        def quantise_y(g, half):
+            if half == 0:
+                live["y_codes", g] = work.tile([P, N], U32, name="y_codes", tag="y_codes", bufs=2, align_bytes=64)
+                live["y_scales", g] = work.tile([P, N], U8, name="y_scales", tag="y_scales", bufs=2, align_bytes=64)
+            cols = slice(256 * half, 256 * half + 256)
             nc.vector.quantize_mx(
-                out=live["y_codes", g][:].bitcast(FP8X4), scales=live["y_scales", g][:], in_=live["y_grouped", g][:]
+                out=live["y_codes", g][:, cols].bitcast(FP8X4),
+                scales=live["y_scales", g][:, cols],
+                in_=live["y_grouped", g][:, 1024 * half : 1024 * half + 1024],
             )
 
         def project(x):
@@ -180,7 +184,7 @@ def tile_blockgrucell_pb_t_kernel(tc, y_dyn, deter, gru_W, gru_b, out):
                 in1=live["deterT", x // 2][:].bitcast(BF16).rearrange("p (n e) -> p e n", e=2)[:, x % 2, :],
                 op=ALU.subtract,
             )
-            engine = nc.vector if x % 4 == 3 else nc.gpsimd
+            engine = nc.vector if x == STRIPS - 1 else nc.gpsimd
             engine.tensor_tensor(out=live["step", x][:], in0=live["update", x][:], in1=live["diff", x][:], op=ALU.mult)
 
         def transpose_back(x):
@@ -210,7 +214,8 @@ def tile_blockgrucell_pb_t_kernel(tc, y_dyn, deter, gru_W, gru_b, out):
         regroup_y(0, 1)
         regroup_weights(nc.vector.tensor_copy, 0, GATE_R)
         quantise_weights(0, GATE_R)
-        quantise_y(0)
+        quantise_y(0, 0)
+        quantise_y(0, 1)
         regroup_weights(nc.scalar.copy, 0, GATE_U)
         regroup_weights(nc.vector.tensor_copy, 0, GATE_C)
         quantise_weights(0, GATE_U)
@@ -225,8 +230,8 @@ def tile_blockgrucell_pb_t_kernel(tc, y_dyn, deter, gru_W, gru_b, out):
         for s in range(-2, STRIPS + 4):
             if in_range(s - 1):
                 blend(s - 1)
-            if 4 <= s + 3 < STRIPS and (s + 3) % 4 == 0:
-                quantise_y((s + 3) // 4)
+            if 4 <= s + 4 < STRIPS and (s + 4) % 4 < 2:
+                quantise_y((s + 4) // 4, (s + 4) % 4)
             if in_range(s + 1):
                 gates(s + 1)
             if 4 <= s + 5 < STRIPS and (s + 5) % 4 < 2:

from contextlib import ExitStack

import concourse.mybir as mybir
from concourse.masks import make_identity

FLOPS = 2 * 4096 * 512 * 1536

F32 = mybir.dt.float32
BF16 = mybir.dt.bfloat16
U32 = mybir.dt.uint32
U8 = mybir.dt.uint8
FP8X4 = mybir.dt.float8_e4m3fn_x4
ACT = mybir.ActivationFunctionType
ALU = mybir.AluOpType

P = 128
N = 512
ROUNDS = 8
STRIPS = 4 * ROUNDS
GATE_R, GATE_C, GATE_U = 0, 1, 2


def tile_blockgrucell_pb_t_kernel(tc, y_dyn, deter, gru_W, gru_b, out):
    nc = tc.nc
    y_rows = y_dyn.rearrange("(g p i) k -> g p (i k)", p=P, i=4)
    d_rows = deter.rearrange("(g p i) c -> g p (i c)", p=P, i=4)
    o_rows = out.rearrange("(g p i) c -> g p i c", p=P, i=4)

    with ExitStack() as ctx:
        keep = ctx.enter_context(tc.tile_pool(name="keep", bufs=1))
        work = ctx.enter_context(tc.tile_pool(name="work", bufs=3))
        psum = ctx.enter_context(tc.psum_pool(name="psum", bufs=1))
        ctx.enter_context(tc.manual_schedule())

        def bank(tag, bufs):
            return psum.tile([P, N], F32, name=tag, tag=tag, bufs=bufs)

        def strip_tile(tag, bufs):
            return work.tile([P, N], F32, name=tag, tag=tag, bufs=bufs)

        ident = keep.tile([P, P], F32, name="ident")
        make_identity(nc, ident[:])
        b_rows = keep.tile([P, 256], BF16, name="b_rows")
        nc.vector.memset(b_rows[:], 0.0)
        nc.scalar.dma_start(out=b_rows[0:6, :], in_=gru_b.rearrange("(m c) -> m c", c=256))
        warm = keep.tile([P, 2], F32, name="warm")
        nc.vector.memset(warm[:], 0.0)
        nc.scalar.activation(out=warm[:, 1:2], in_=warm[:, 0:1], func=ACT.Sigmoid)

        y_sb = [keep.tile([P, 4 * 512], BF16, name="y%d" % g) for g in range(ROUNDS)]
        d_sb = [keep.tile([P, 4 * 512], BF16, name="d%d" % g) for g in range(ROUNDS)]
        w_raw = keep.tile([P, 4, 1536], BF16, name="w_raw")
        for half in range(2):
            cols = slice(1024 * half, 1024 * half + 1024)
            nc.sync.dma_start(out=y_sb[0][:, cols], in_=y_rows[0][:, cols])
        for h in range(2):
            for gate in (GATE_R, GATE_U, GATE_C):
                cols = slice(512 * gate + 256 * h, 512 * gate + 256 * h + 256)
                for u in range(2):
                    nc.sync.dma_start(
                        out=w_raw[:, 2 * u : 2 * u + 2, cols],
                        in_=gru_W[0, 256 * u : 256 * u + 256, cols].rearrange("(q j) c -> q j c", j=2),
                    )
        for g in range(ROUNDS):
            if g + 1 < ROUNDS:
                nc.sync.dma_start(out=y_sb[g + 1][:], in_=y_rows[g + 1])
            nc.sync.dma_start(out=d_sb[g][:], in_=d_rows[g])

        b_bank = bank("yT", 1)
        nc.tensor.transpose(b_bank[:, 0:P], b_rows[:].bitcast(F32), ident[:])
        bias = keep.tile([P, 12], F32, name="bias")
        nc.vector.tensor_copy(out=bias[:], in_=b_bank[:].bitcast(BF16)[:, 0:12])
        nc.vector.tensor_scalar_add(
            out=bias[:, 4 * GATE_U : 4 * GATE_U + 4], in0=bias[:, 4 * GATE_U : 4 * GATE_U + 4], scalar1=-1.0
        )

        def bias_of(gate, x):
            column = 4 * gate + x % 4
            return bias[:, column : column + 1]

        w_grouped = keep.tile([P, 6 * 1024], BF16, name="w_grouped", align_bytes=64)
        w_codes = keep.tile([P, 6 * 256], U32, name="w_codes", align_bytes=64)
        w_scales = keep.tile([P, 6 * 256], U8, name="w_scales", align_bytes=64)

        def regroup_weights(copy, h, gate):
            slot = 3 * h + gate
            first = 512 * gate + 256 * h
            copy(
                out=w_grouped[:, 1024 * slot : 1024 * slot + 1024].rearrange("p (e q t) -> p e q t", e=2, t=4),
                in_=w_raw[:, :, first : first + 256].rearrange("p t (q e) -> p e q t", e=2),
            )

        def quantise_weights(h, gate):
            slot = 3 * h + gate
            nc.vector.quantize_mx(
                out=w_codes[:, 256 * slot : 256 * slot + 256].bitcast(FP8X4),
                scales=w_scales[:, 256 * slot : 256 * slot + 256],
                in_=w_grouped[:, 1024 * slot : 1024 * slot + 1024],
            )

        live = {}

        def transpose_y(g, half):
            live["yT", g, half] = bank("back", 2) if g == 0 else bank("yT", 1)
            words = y_sb[g][:].bitcast(F32)
            for i in range(2):
                for u in range(2):
                    src = 256 * (2 * half + i) + 128 * u
                    dst = 128 * (2 * i + u)
                    nc.tensor.transpose(live["yT", g, half][:, dst : dst + P], words[:, src : src + P], ident[:])

        def regroup_y(g, half):
            if half == 0:
                live["y_grouped", g] = work.tile([P, 4 * N], BF16, name="y_grouped", tag="y_grouped", bufs=2, align_bytes=64)
            words = live["y_grouped", g][:].bitcast(F32).rearrange("p (n u) -> p n u", u=2)
            nc.scalar.copy(
                out=words[:, 256 * half : 256 * half + 256, :].rearrange("p (i r) u -> p i r u", i=2),
                in_=live["yT", g, half][:].rearrange("p (i u r) -> p i r u", i=2, u=2),
            )

        def quantise_y(g, half):
            if half == 0:
                live["y_codes", g] = work.tile([P, N], U32, name="y_codes", tag="y_codes", bufs=2, align_bytes=64)
                live["y_scales", g] = work.tile([P, N], U8, name="y_scales", tag="y_scales", bufs=2, align_bytes=64)
            cols = slice(256 * half, 256 * half + 256)
            nc.vector.quantize_mx(
                out=live["y_codes", g][:, cols].bitcast(FP8X4),
                scales=live["y_scales", g][:, cols],
                in_=live["y_grouped", g][:, 1024 * half : 1024 * half + 1024],
            )

        def project(x):
            g, h, e = x // 4, x // 2 % 2, x % 2
            for gate in (GATE_R, GATE_U, GATE_C):
                first = 256 * (3 * h + gate) + P * e
                live["z", gate, x] = bank("z", 4)
                nc.tensor.matmul_mx(
                    out=live["z", gate, x][:],
                    lhsT=w_codes[:, first : first + P].bitcast(FP8X4),
                    lhsT_scale=w_scales[:, first : first + P],
                    rhs=live["y_codes", g][:].bitcast(FP8X4),
                    rhs_scale=live["y_scales", g][:],
                    start=True,
                    stop=True,
                )

        def gates(x):
            live["reset", x] = strip_tile("reset", 3)
            live["update", x] = strip_tile("update", 5)
            live["product", x] = strip_tile("product", 3)
            nc.scalar.activation(
                out=live["reset", x][:], in_=live["z", GATE_R, x][:], func=ACT.Sigmoid, bias=bias_of(GATE_R, x)
            )
            nc.scalar.activation(
                out=live["update", x][:], in_=live["z", GATE_U, x][:], func=ACT.Sigmoid, bias=bias_of(GATE_U, x)
            )
            nc.vector.scalar_tensor_tensor(
                out=live["product", x][:],
                in0=live["z", GATE_C, x][:],
                scalar=bias_of(GATE_C, x),
                in1=live["reset", x][:],
                op0=ALU.add,
                op1=ALU.mult,
            )

        def candidate(x):
            live["cand", x] = strip_tile("cand", 3)
            nc.scalar.activation(out=live["cand", x][:], in_=live["product", x][:], func=ACT.Tanh)

        def transpose_deter(pair):
            g, h = pair // 2, pair % 2
            live["deterT", pair] = bank("deterT", 1)
            words = d_sb[g][:].bitcast(F32)
            for i in range(4):
                src = 256 * i + P * h
                nc.tensor.transpose(live["deterT", pair][:, P * i : P * i + P], words[:, src : src + P], ident[:])

        def blend(x):
            live["diff", x] = strip_tile("diff", 3)
            live["step", x] = strip_tile("step", 5)
            nc.vector.tensor_tensor(
                out=live["diff", x][:],
                in0=live["cand", x][:],
                in1=live["deterT", x // 2][:].bitcast(BF16).rearrange("p (n e) -> p e n", e=2)[:, x % 2, :],
                op=ALU.subtract,
            )
            engine = nc.vector if x == STRIPS - 1 else nc.gpsimd
            engine.tensor_tensor(out=live["step", x][:], in0=live["update", x][:], in1=live["diff", x][:], op=ALU.mult)

        def transpose_back(x):
            even = x - x % 2
            live["back", x] = bank("back", 2)
            for i in range(2):
                for e in range(2):
                    src = P * (2 * (x % 2) + i)
                    dst = P * (2 * i + e)
                    nc.tensor.transpose(live["back", x][:, dst : dst + P], live["step", even + e][:, src : src + P], ident[:])

        def finish(x):
            g, h, slots = x // 4, x // 2 % 2, slice(2 * (x % 2), 2 * (x % 2) + 2)
            cols = slice(256 * h, 256 * h + 256)
            result = strip_tile("result", 4)
            nc.vector.tensor_tensor(
                out=result[:].rearrange("p (i q e) -> p i q e", i=2, e=2),
                in0=live["back", x][:].rearrange("p (i e q) -> p i q e", i=2, e=2),
                in1=d_sb[g][:].rearrange("p (i c) -> p i c", i=4)[:, slots, cols].rearrange("p i (q e) -> p i q e", e=2),
                op=ALU.add,
            )
            nc.sync.dma_start(out=o_rows[g][:, slots, cols], in_=result[:].rearrange("p (i c) -> p i c", i=2))

        transpose_y(0, 0)
        transpose_y(0, 1)
        regroup_y(0, 0)
        regroup_y(0, 1)
        regroup_weights(nc.vector.tensor_copy, 0, GATE_R)
        quantise_weights(0, GATE_R)
        quantise_y(0, 0)
        quantise_y(0, 1)
        regroup_weights(nc.scalar.copy, 0, GATE_U)
        regroup_weights(nc.vector.tensor_copy, 0, GATE_C)
        quantise_weights(0, GATE_U)
        quantise_weights(0, GATE_C)
        for gate in (GATE_R, GATE_U, GATE_C):
            regroup_weights(nc.vector.tensor_copy, 1, gate)
            quantise_weights(1, gate)

        def in_range(x):
            return 0 <= x < STRIPS

        for s in range(-2, STRIPS + 4):
            if in_range(s - 1):
                blend(s - 1)
            if 4 <= s + 4 < STRIPS and (s + 4) % 4 < 2:
                quantise_y((s + 4) // 4, (s + 4) % 4)
            if in_range(s + 1):
                gates(s + 1)
            if 4 <= s + 5 < STRIPS and (s + 5) % 4 < 2:
                regroup_y((s + 5) // 4, (s + 5) % 4)
            if in_range(s - 4):
                finish(s - 4)
            if in_range(s):
                candidate(s)
            if in_range(s + 2):
                project(s + 2)
            if 4 <= s + 6 < STRIPS and (s + 6) % 4 < 2:
                transpose_y((s + 6) // 4, (s + 6) % 4)
            if in_range(s) and s % 2 == 0:
                transpose_deter(s // 2)
            if in_range(s - 3):
                transpose_back(s - 3)
